import numpy as np
import ml_dtypes

BF16 = ml_dtypes.bfloat16


def bf(x):
    return np.asarray(x, np.float32).astype(BF16)


def f32(x):
    return np.asarray(x, np.float32)


def f64(x):
    return np.asarray(x).astype(np.float64)


def striped(idx):
    return np.tile(idx.reshape(-1, 16).T, (8, 1))


C, S, H, SIDES, K, B, N, L2, L3 = 256, 1024, 512, 2, 8, 512, 8192, 2048, 2048


def crelu(v):
    return np.minimum(np.maximum(v, 0.0), 1.0)


def setup_inputs():
    return {
        "table": f32(0.2 * np.random.standard_normal((C, S))),
        "ft_bias": f32(0.1 * np.random.standard_normal((C, 1))),
        "stm": f32(np.random.uniform(0.0, 1.0, (1, B))),
        "w1a": bf(1.5 * np.random.standard_normal((C, L2)) / np.sqrt(SIDES * C)),
        "w1b": bf(1.5 * np.random.standard_normal((C, L2)) / np.sqrt(SIDES * C)),
        "b1": f32(0.1 * np.random.standard_normal((L2, 1))),
        "w2": bf(1.5 * np.random.standard_normal((L2, L3)) / np.sqrt(L2)),
        "b2": f32(0.1 * np.random.standard_normal((L3, 1))),
        "offs": striped(np.concatenate([np.random.permutation(S)[:H] for _ in range(SIDES * K)])),
    }


def reference(table, ft_bias, stm, w1a, w1b, b1, w2, b2, offs):
    idx = offs[:16].T.reshape(-1)
    bags = f64(table)[:, idx].reshape(C, SIDES, K, B).sum(axis=2) + f64(ft_bias)[:, :, None]
    wacc, bacc = bags[:, 0], bags[:, 1]
    s = f64(stm)
    xa = crelu(s * wacc + (1.0 - s) * bacc)
    xb = crelu(s * bacc + (1.0 - s) * wacc)
    h1 = crelu(f64(w1a).T @ xa + f64(w1b).T @ xb + f64(b1))
    return crelu(f64(w2).T @ h1 + f64(b2))

@@ -1,0 +1,120 @@
+import concourse.mybir as mybir
+
+F32 = mybir.dt.float32
+BF16 = mybir.dt.bfloat16
+U16 = mybir.dt.uint16
+ADD = mybir.AluOpType.add
+SUBTRACT = mybir.AluOpType.subtract
+MULT = mybir.AluOpType.mult
+MAX = mybir.AluOpType.max
+MIN = mybir.AluOpType.min
+RELU = mybir.ActivationFunctionType.Relu
+
+P = 128
+C = 256
+S = 1024
+B = 512
+SLOTS = 8
+L2 = 2048
+L3 = 2048
+CB = C // P
+MB = L2 // P
+QB = L3 // P
+PW = 512
+W2_PIECES = 4
+QB_PER_PIECE = QB // W2_PIECES
+
+FLOPS = 2 * B * (2 * C * L2 + L2 * L3)
+
+
+def tile_halfkpnnue_b_kernel(tc, table, ft_bias, stm, w1a, w1b, b1, w2, b2, offs, out):
+    nc = tc.nc
+    with (
+        tc.tile_pool(name="held", bufs=1) as held,
+        tc.tile_pool(name="sums", bufs=6) as sums,
+        tc.tile_pool(name="work", bufs=2) as work,
+        tc.tile_pool(name="acts", bufs=2) as acts,
+        tc.tile_pool(name="stage", bufs=8) as stage,
+        tc.psum_pool(name="psum", bufs=8) as psum,
+    ):
+        offsets = held.tile([P, SLOTS * 2 * B // 16], U16, name="offsets")
+        nc.sync.dma_start(offsets[:], offs)
+        table_sb = []
+        for cb in range(CB):
+            block = held.tile([P, S], F32, name="table%d" % cb)
+            nc.sync.dma_start(block[:], table[cb * P : (cb + 1) * P, :])
+            table_sb.append(block)
+        w1a_sb = held.tile([P, CB, L2], BF16, name="w1a_sb")
+        nc.sync.dma_start(w1a_sb[:], w1a.rearrange("(cb p) m -> p cb m", p=P))
+        w1b_sb = held.tile([P, CB, L2], BF16, name="w1b_sb")
+        nc.sync.dma_start(w1b_sb[:], w1b.rearrange("(cb p) m -> p cb m", p=P))
+        w2_rows = w2.rearrange("(mb p) q -> p mb q", p=P)
+        w2_sb = []
+        for j in range(W2_PIECES):
+            piece = held.tile([P, MB, L3 // W2_PIECES], BF16, name="w2_%d" % j)
+            nc.sync.dma_start(piece[:], w2_rows[:, :, j * (L3 // W2_PIECES) : (j + 1) * (L3 // W2_PIECES)])
+            w2_sb.append(piece)
+
+        ft_sb = held.tile([P, CB], F32, name="ft_sb")
+        b1_sb = held.tile([P, MB], F32, name="b1_sb")
+        b2_sb = held.tile([P, QB], F32, name="b2_sb")
+        stm_sb = held.tile([P, B], F32, name="stm_sb")
+        with nc.allow_non_contiguous_dma(reason="one bias value to a partition"):
+            nc.scalar.dma_start(ft_sb[:], ft_bias.rearrange("(a p) o -> p (a o)", p=P))
+            nc.scalar.dma_start(stm_sb[:], stm.rearrange("o b -> (o b)").partition_broadcast(P))
+            nc.scalar.dma_start(b1_sb[:], b1.rearrange("(a p) o -> p (a o)", p=P))
+            nc.scalar.dma_start(b2_sb[:], b2.rearrange("(a p) o -> p (a o)", p=P))
+
+        bias_start = []
+        for cb in range(CB):
+            spread = held.tile([P, PW], F32, name="bias_start%d" % cb)
+            nc.vector.tensor_copy(spread[:], ft_sb[:, cb : cb + 1].to_broadcast([P, PW]))
+            bias_start.append(spread)
+
+        def gather_bag(side, cb, p0):
+            running = bias_start[cb]
+            for t in range(SLOTS):
+                first = ((side * SLOTS + t) * B + p0) // 16
+                picked = table_sb[cb][:].indirect(offsets[:, first : first + PW // 16])
+                longer = sums.tile([P, PW], F32, name="bag")
+                nc.vector.tensor_tensor(longer[:], picked, running[:], ADD)
+                running = longer
+            return running
+
+        for p0 in range(0, B, PW):
+            xa = acts.tile([P, CB, PW], BF16, name="xa")
+            xb = acts.tile([P, CB, PW], BF16, name="xb")
+            for cb in range(CB):
+                wacc = gather_bag(0, cb, p0)
+                bacc = gather_bag(1, cb, p0)
+                lean = work.tile([P, PW], F32, name="lean")
+                nc.vector.tensor_tensor(lean[:], wacc[:], bacc[:], SUBTRACT)
+                nc.vector.tensor_tensor(lean[:], lean[:], stm_sb[:, p0 : p0 + PW], MULT)
+                ya = work.tile([P, PW], F32, name="ya")
+                nc.vector.tensor_tensor(ya[:], bacc[:], lean[:], ADD)
+                yb = work.tile([P, PW], F32, name="yb")
+                nc.vector.tensor_tensor(yb[:], wacc[:], lean[:], SUBTRACT)
+                nc.vector.tensor_scalar(xa[:, cb, :], ya[:], 0.0, 1.0, MAX, MIN)
+                nc.vector.tensor_scalar(xb[:, cb, :], yb[:], 0.0, 1.0, MAX, MIN)
+
+            h1 = acts.tile([P, MB, PW], BF16, name="h1")
+            for mb in range(MB):
+                units = slice(mb * P, (mb + 1) * P)
+                acc = psum.tile([P, PW], F32, name="acc")
+                for cb in range(CB):
+                    nc.tensor.matmul(acc[:], w1a_sb[:, cb, units], xa[:, cb, :], start=(cb == 0), stop=False)
+                for cb in range(CB):
+                    nc.tensor.matmul(acc[:], w1b_sb[:, cb, units], xb[:, cb, :], start=False, stop=(cb == CB - 1))
+                nc.scalar.activation(h1[:, mb, :], acc[:], RELU, bias=b1_sb[:, mb : mb + 1])
+                nc.vector.tensor_scalar_min(h1[:, mb, :], h1[:, mb, :], 1.0)
+
+            for qb in range(QB):
+                piece = w2_sb[qb // QB_PER_PIECE]
+                units = slice((qb % QB_PER_PIECE) * P, (qb % QB_PER_PIECE + 1) * P)
+                acc = psum.tile([P, PW], F32, name="acc")
+                for mb in range(MB):
+                    nc.tensor.matmul(acc[:], piece[:, mb, units], h1[:, mb, :], start=(mb == 0), stop=(mb == MB - 1))
+                res = stage.tile([P, PW], F32, name="res")
+                nc.scalar.activation(res[:], acc[:], RELU, bias=b2_sb[:, qb : qb + 1])
+                nc.vector.tensor_scalar_min(res[:], res[:], 1.0)
+                nc.sync.dma_start(out[qb * P : (qb + 1) * P, p0 : p0 + PW], res[:])

@@ -20,7 +20,7 @@ L3 = 2048
 CB = C // P
 MB = L2 // P
 QB = L3 // P
-PW = 512
+PW = 128
 W2_PIECES = 4
 QB_PER_PIECE = QB // W2_PIECES
 
@@ -34,7 +34,7 @@ def tile_halfkpnnue_b_kernel(tc, table, ft_bias, stm, w1a, w1b, b1, w2, b2, offs
         tc.tile_pool(name="sums", bufs=6) as sums,
         tc.tile_pool(name="work", bufs=2) as work,
         tc.tile_pool(name="acts", bufs=2) as acts,
-        tc.tile_pool(name="stage", bufs=8) as stage,
+        tc.tile_pool(name="stage", bufs=16) as stage,
         tc.psum_pool(name="psum", bufs=8) as psum,
     ):
         offsets = held.tile([P, SLOTS * 2 * B // 16], U16, name="offsets")
@@ -81,7 +81,7 @@ def tile_halfkpnnue_b_kernel(tc, table, ft_bias, stm, w1a, w1b, b1, w2, b2, offs
                 running = longer
             return running
 
-        for p0 in range(0, B, PW):
+        def blended_inputs(p0):
             xa = acts.tile([P, CB, PW], BF16, name="xa")
             xb = acts.tile([P, CB, PW], BF16, name="xb")
             for cb in range(CB):
@@ -96,7 +96,9 @@ def tile_halfkpnnue_b_kernel(tc, table, ft_bias, stm, w1a, w1b, b1, w2, b2, offs
                 nc.vector.tensor_tensor(yb[:], wacc[:], lean[:], SUBTRACT)
                 nc.vector.tensor_scalar(xa[:, cb, :], ya[:], 0.0, 1.0, MAX, MIN)
                 nc.vector.tensor_scalar(xb[:, cb, :], yb[:], 0.0, 1.0, MAX, MIN)
+            return xa, xb
 
+        def first_layer(xa, xb):
             h1 = acts.tile([P, MB, PW], BF16, name="h1")
             for mb in range(MB):
                 units = slice(mb * P, (mb + 1) * P)
@@ -107,7 +109,9 @@ def tile_halfkpnnue_b_kernel(tc, table, ft_bias, stm, w1a, w1b, b1, w2, b2, offs
                     nc.tensor.matmul(acc[:], w1b_sb[:, cb, units], xb[:, cb, :], start=False, stop=(cb == CB - 1))
                 nc.scalar.activation(h1[:, mb, :], acc[:], RELU, bias=b1_sb[:, mb : mb + 1])
                 nc.vector.tensor_scalar_min(h1[:, mb, :], h1[:, mb, :], 1.0)
+            return h1
 
+        def second_layer(h1, p0):
             for qb in range(QB):
                 piece = w2_sb[qb // QB_PER_PIECE]
                 units = slice((qb % QB_PER_PIECE) * P, (qb % QB_PER_PIECE + 1) * P)
@@ -118,3 +122,10 @@ def tile_halfkpnnue_b_kernel(tc, table, ft_bias, stm, w1a, w1b, b1, w2, b2, offs
                 nc.scalar.activation(res[:], acc[:], RELU, bias=b2_sb[:, qb : qb + 1])
                 nc.vector.tensor_scalar_min(res[:], res[:], 1.0)
                 nc.sync.dma_start(out[qb * P : (qb + 1) * P, p0 : p0 + PW], res[:])
+
+        inputs = blended_inputs(0)
+        for p0 in range(0, B, PW):
+            h1 = first_layer(inputs[0], inputs[1])
+            if p0 + PW < B:
+                inputs = blended_inputs(p0 + PW)
+            second_layer(h1, p0)

@@ -1,4 +1,5 @@
 import concourse.mybir as mybir
+from concourse.masks import make_identity
 
 F32 = mybir.dt.float32
 BF16 = mybir.dt.bfloat16
@@ -9,11 +10,13 @@ MULT = mybir.AluOpType.mult
 MAX = mybir.AluOpType.max
 MIN = mybir.AluOpType.min
 RELU = mybir.ActivationFunctionType.Relu
+COPY = mybir.ActivationFunctionType.Copy
 
 P = 128
 C = 256
 S = 1024
 B = 512
+SIDES = 2
 SLOTS = 8
 L2 = 2048
 L3 = 2048
@@ -23,6 +26,7 @@ QB = L3 // P
 PW = 128
 W2_PIECES = 4
 QB_PER_PIECE = QB // W2_PIECES
+BIAS_ROWS = 64
 
 FLOPS = 2 * B * (2 * C * L2 + L2 * L3)
 
@@ -31,23 +35,32 @@ def tile_halfkpnnue_b_kernel(tc, table, ft_bias, stm, w1a, w1b, b1, w2, b2, offs
     nc = tc.nc
     with (
         tc.tile_pool(name="held", bufs=1) as held,
-        tc.tile_pool(name="sums", bufs=6) as sums,
+        tc.tile_pool(name="sums", bufs=3) as sums,
         tc.tile_pool(name="work", bufs=2) as work,
         tc.tile_pool(name="acts", bufs=2) as acts,
-        tc.tile_pool(name="stage", bufs=16) as stage,
+        tc.tile_pool(name="rooms", bufs=4) as rooms,
+        tc.tile_pool(name="stage", bufs=8) as stage,
         tc.psum_pool(name="psum", bufs=8) as psum,
     ):
-        offsets = held.tile([P, SLOTS * 2 * B // 16], U16, name="offsets")
+        offsets = held.tile([P, SIDES * SLOTS * B // 16], U16, name="offsets")
         nc.sync.dma_start(offsets[:], offs)
+        ft_sb = held.tile([P, CB], F32, name="ft_sb")
+        with nc.allow_non_contiguous_dma(reason="256 values, one to a partition"):
+            nc.sync.dma_start(ft_sb[:], ft_bias.rearrange("(a p) o -> p (a o)", p=P))
         table_sb = []
         for cb in range(CB):
             block = held.tile([P, S], F32, name="table%d" % cb)
             nc.sync.dma_start(block[:], table[cb * P : (cb + 1) * P, :])
             table_sb.append(block)
+        stm_sb = held.tile([P, B], F32, name="stm_sb")
+        nc.sync.dma_start(stm_sb[:], stm.rearrange("o b -> (o b)").partition_broadcast(P))
         w1a_sb = held.tile([P, CB, L2], BF16, name="w1a_sb")
         nc.sync.dma_start(w1a_sb[:], w1a.rearrange("(cb p) m -> p cb m", p=P))
         w1b_sb = held.tile([P, CB, L2], BF16, name="w1b_sb")
         nc.sync.dma_start(w1b_sb[:], w1b.rearrange("(cb p) m -> p cb m", p=P))
+        bias_rows = held.tile([BIAS_ROWS, P], F32, name="bias_rows")
+        nc.sync.dma_start(bias_rows[0:MB, :], b1.rearrange("(a p) o -> a (p o)", p=P))
+        nc.sync.dma_start(bias_rows[MB : MB + QB, :], b2.rearrange("(a p) o -> a (p o)", p=P))
         w2_rows = w2.rearrange("(mb p) q -> p mb q", p=P)
         w2_sb = []
         for j in range(W2_PIECES):
@@ -55,15 +68,20 @@ def tile_halfkpnnue_b_kernel(tc, table, ft_bias, stm, w1a, w1b, b1, w2, b2, offs
             nc.sync.dma_start(piece[:], w2_rows[:, :, j * (L3 // W2_PIECES) : (j + 1) * (L3 // W2_PIECES)])
             w2_sb.append(piece)
 
-        ft_sb = held.tile([P, CB], F32, name="ft_sb")
-        b1_sb = held.tile([P, MB], F32, name="b1_sb")
-        b2_sb = held.tile([P, QB], F32, name="b2_sb")
-        stm_sb = held.tile([P, B], F32, name="stm_sb")
-        with nc.allow_non_contiguous_dma(reason="one bias value to a partition"):
-            nc.scalar.dma_start(ft_sb[:], ft_bias.rearrange("(a p) o -> p (a o)", p=P))
-            nc.scalar.dma_start(stm_sb[:], stm.rearrange("o b -> (o b)").partition_broadcast(P))
-            nc.scalar.dma_start(b1_sb[:], b1.rearrange("(a p) o -> p (a o)", p=P))
-            nc.scalar.dma_start(b2_sb[:], b2.rearrange("(a p) o -> p (a o)", p=P))
+        nc.gpsimd.memset(bias_rows[MB + QB : BIAS_ROWS, :], 0.0)
+        identity = held.tile([BIAS_ROWS, BIAS_ROWS], F32, name="identity")
+        make_identity(nc, identity[:])
+        bias_ps = psum.tile([P, BIAS_ROWS], F32, tag="acc")
+        nc.tensor.transpose(bias_ps[:], bias_rows[:], identity[:])
+        one_less_bias = held.tile([P, BIAS_ROWS], F32, name="one_less_bias")
+        nc.scalar.activation(one_less_bias[:], bias_ps[:], COPY, bias=1.0, scale=-1.0)
+        one_less_b1 = one_less_bias[:, 0:MB]
+        one_less_b2 = one_less_bias[:, MB : MB + QB]
+
+        def clip_out_of_psum(clipped, acc, one_less_b):
+            room = rooms.tile([P, PW], F32, name="room")
+            nc.scalar.activation(room[:], acc[:], RELU, bias=one_less_b, scale=-1.0)
+            nc.scalar.activation(clipped, room[:], RELU, bias=1.0, scale=-1.0)
 
         bias_start = []
         for cb in range(CB):
@@ -71,31 +89,32 @@ def tile_halfkpnnue_b_kernel(tc, table, ft_bias, stm, w1a, w1b, b1, w2, b2, offs
             nc.vector.tensor_copy(spread[:], ft_sb[:, cb : cb + 1].to_broadcast([P, PW]))
             bias_start.append(spread)
 
-        def gather_bag(side, cb, p0):
-            running = bias_start[cb]
-            for t in range(SLOTS):
-                first = ((side * SLOTS + t) * B + p0) // 16
-                picked = table_sb[cb][:].indirect(offsets[:, first : first + PW // 16])
-                longer = sums.tile([P, PW], F32, name="bag")
-                nc.vector.tensor_tensor(longer[:], picked, running[:], ADD)
-                running = longer
-            return running
-
         def blended_inputs(p0):
+            bags = [[bias_start[cb] for cb in range(CB)] for side in range(SIDES)]
+            for t in range(SLOTS):
+                for side in range(SIDES):
+                    first = ((side * SLOTS + t) * B + p0) // 16
+                    for cb in range(CB):
+                        picked = table_sb[cb][:].indirect(offsets[:, first : first + PW // 16])
+                        longer = sums.tile([P, PW], F32, name="bag%d%d" % (side, cb))
+                        nc.vector.tensor_tensor(longer[:], picked, bags[side][cb][:], ADD)
+                        bags[side][cb] = longer
+            wacc, bacc = bags
+            lean = [work.tile([P, PW], F32, name="lean%d" % cb) for cb in range(CB)]
+            ya = [work.tile([P, PW], F32, name="ya%d" % cb) for cb in range(CB)]
+            yb = [work.tile([P, PW], F32, name="yb%d" % cb) for cb in range(CB)]
             xa = acts.tile([P, CB, PW], BF16, name="xa")
             xb = acts.tile([P, CB, PW], BF16, name="xb")
             for cb in range(CB):
-                wacc = gather_bag(0, cb, p0)
-                bacc = gather_bag(1, cb, p0)
-                lean = work.tile([P, PW], F32, name="lean")
-                nc.vector.tensor_tensor(lean[:], wacc[:], bacc[:], SUBTRACT)
-                nc.vector.tensor_tensor(lean[:], lean[:], stm_sb[:, p0 : p0 + PW], MULT)
-                ya = work.tile([P, PW], F32, name="ya")
-                nc.vector.tensor_tensor(ya[:], bacc[:], lean[:], ADD)
-                yb = work.tile([P, PW], F32, name="yb")
-                nc.vector.tensor_tensor(yb[:], wacc[:], lean[:], SUBTRACT)
-                nc.vector.tensor_scalar(xa[:, cb, :], ya[:], 0.0, 1.0, MAX, MIN)
-                nc.vector.tensor_scalar(xb[:, cb, :], yb[:], 0.0, 1.0, MAX, MIN)
+                nc.vector.tensor_tensor(lean[cb][:], wacc[cb][:], bacc[cb][:], SUBTRACT)
+            for cb in range(CB):
+                nc.vector.tensor_tensor(lean[cb][:], lean[cb][:], stm_sb[:, p0 : p0 + PW], MULT)
+            for cb in range(CB):
+                nc.vector.tensor_tensor(ya[cb][:], bacc[cb][:], lean[cb][:], ADD)
+                nc.vector.tensor_tensor(yb[cb][:], wacc[cb][:], lean[cb][:], SUBTRACT)
+            for cb in range(CB):
+                nc.vector.tensor_scalar(xa[:, cb, :], ya[cb][:], 0.0, 1.0, MAX, MIN)
+                nc.vector.tensor_scalar(xb[:, cb, :], yb[cb][:], 0.0, 1.0, MAX, MIN)
             return xa, xb
 
         def first_layer(xa, xb):
@@ -107,8 +126,7 @@ def tile_halfkpnnue_b_kernel(tc, table, ft_bias, stm, w1a, w1b, b1, w2, b2, offs
                     nc.tensor.matmul(acc[:], w1a_sb[:, cb, units], xa[:, cb, :], start=(cb == 0), stop=False)
                 for cb in range(CB):
                     nc.tensor.matmul(acc[:], w1b_sb[:, cb, units], xb[:, cb, :], start=False, stop=(cb == CB - 1))
-                nc.scalar.activation(h1[:, mb, :], acc[:], RELU, bias=b1_sb[:, mb : mb + 1])
-                nc.vector.tensor_scalar_min(h1[:, mb, :], h1[:, mb, :], 1.0)
+                clip_out_of_psum(h1[:, mb, :], acc, one_less_b1[:, mb : mb + 1])
             return h1
 
         def second_layer(h1, p0):
@@ -119,8 +137,7 @@ def tile_halfkpnnue_b_kernel(tc, table, ft_bias, stm, w1a, w1b, b1, w2, b2, offs
                 for mb in range(MB):
                     nc.tensor.matmul(acc[:], piece[:, mb, units], h1[:, mb, :], start=(mb == 0), stop=(mb == MB - 1))
                 res = stage.tile([P, PW], F32, name="res")
-                nc.scalar.activation(res[:], acc[:], RELU, bias=b2_sb[:, qb : qb + 1])
-                nc.vector.tensor_scalar_min(res[:], res[:], 1.0)
+                clip_out_of_psum(res[:], acc, one_less_b2[:, qb : qb + 1])
                 nc.sync.dma_start(out[qb * P : (qb + 1) * P, p0 : p0 + PW], res[:])
 
         inputs = blended_inputs(0)

@@ -23,7 +23,10 @@ L3 = 2048
 CB = C // P
 MB = L2 // P
 QB = L3 // P
-PW = 128
+WIDTHS = (96, 96, 128, 192)
+LAG = 2
+WIDEST = max(WIDTHS)
+assert sum(WIDTHS) == B
 W2_PIECES = 4
 QB_PER_PIECE = QB // W2_PIECES
 BIAS_ROWS = 64
@@ -35,8 +38,7 @@ def tile_halfkpnnue_b_kernel(tc, table, ft_bias, stm, w1a, w1b, b1, w2, b2, offs
     nc = tc.nc
     with (
         tc.tile_pool(name="held", bufs=1) as held,
-        tc.tile_pool(name="sums", bufs=3) as sums,
-        tc.tile_pool(name="work", bufs=2) as work,
+        tc.tile_pool(name="ring", bufs=10) as ring,
         tc.tile_pool(name="acts", bufs=2) as acts,
         tc.tile_pool(name="rooms", bufs=4) as rooms,
         tc.tile_pool(name="stage", bufs=8) as stage,
@@ -78,71 +80,86 @@ def tile_halfkpnnue_b_kernel(tc, table, ft_bias, stm, w1a, w1b, b1, w2, b2, offs
         one_less_b1 = one_less_bias[:, 0:MB]
         one_less_b2 = one_less_bias[:, MB : MB + QB]
 
-        def clip_out_of_psum(clipped, acc, one_less_b):
-            room = rooms.tile([P, PW], F32, name="room")
+        def clip_out_of_psum(clipped, acc, one_less_b, pw):
+            room = rooms.tile([P, pw], F32, name="room")
             nc.scalar.activation(room[:], acc[:], RELU, bias=one_less_b, scale=-1.0)
             nc.scalar.activation(clipped, room[:], RELU, bias=1.0, scale=-1.0)
 
         bias_start = []
         for cb in range(CB):
-            spread = held.tile([P, PW], F32, name="bias_start%d" % cb)
-            nc.vector.tensor_copy(spread[:], ft_sb[:, cb : cb + 1].to_broadcast([P, PW]))
+            spread = held.tile([P, WIDEST], F32, name="bias_start%d" % cb)
+            nc.vector.tensor_copy(spread[:], ft_sb[:, cb : cb + 1].to_broadcast([P, WIDEST]))
             bias_start.append(spread)
 
-        def blended_inputs(p0):
-            bags = [[bias_start[cb] for cb in range(CB)] for side in range(SIDES)]
+        def blended_inputs(p0, pw):
+            bags = [[bias_start[cb][:, 0:pw] for cb in range(CB)] for side in range(SIDES)]
             for t in range(SLOTS):
                 for side in range(SIDES):
                     first = ((side * SLOTS + t) * B + p0) // 16
                     for cb in range(CB):
-                        picked = table_sb[cb][:].indirect(offsets[:, first : first + PW // 16])
-                        longer = sums.tile([P, PW], F32, name="bag%d%d" % (side, cb))
-                        nc.vector.tensor_tensor(longer[:], picked, bags[side][cb][:], ADD)
-                        bags[side][cb] = longer
+                        picked = table_sb[cb][:].indirect(offsets[:, first : first + pw // 16])
+                        longer = ring.tile([P, pw], F32, name="longer", tag="vector")
+                        nc.vector.tensor_tensor(longer[:], picked, bags[side][cb], ADD)
+                        bags[side][cb] = longer[:]
             wacc, bacc = bags
-            lean = [work.tile([P, PW], F32, name="lean%d" % cb) for cb in range(CB)]
-            ya = [work.tile([P, PW], F32, name="ya%d" % cb) for cb in range(CB)]
-            yb = [work.tile([P, PW], F32, name="yb%d" % cb) for cb in range(CB)]
-            xa = acts.tile([P, CB, PW], BF16, name="xa")
-            xb = acts.tile([P, CB, PW], BF16, name="xb")
+            lean = [ring.tile([P, pw], F32, name="lean%d" % cb, tag="vector") for cb in range(CB)]
+            ya = [ring.tile([P, pw], F32, name="ya%d" % cb, tag="vector") for cb in range(CB)]
+            yb = [ring.tile([P, pw], F32, name="yb%d" % cb, tag="vector") for cb in range(CB)]
+            xa = acts.tile([P, CB, pw], BF16, name="xa")
+            xb = acts.tile([P, CB, pw], BF16, name="xb")
             for cb in range(CB):
-                nc.vector.tensor_tensor(lean[cb][:], wacc[cb][:], bacc[cb][:], SUBTRACT)
+                nc.vector.tensor_tensor(lean[cb][:], wacc[cb], bacc[cb], SUBTRACT)
             for cb in range(CB):
-                nc.vector.tensor_tensor(lean[cb][:], lean[cb][:], stm_sb[:, p0 : p0 + PW], MULT)
+                nc.vector.tensor_tensor(lean[cb][:], lean[cb][:], stm_sb[:, p0 : p0 + pw], MULT)
             for cb in range(CB):
-                nc.vector.tensor_tensor(ya[cb][:], bacc[cb][:], lean[cb][:], ADD)
-                nc.vector.tensor_tensor(yb[cb][:], wacc[cb][:], lean[cb][:], SUBTRACT)
+                nc.vector.tensor_tensor(ya[cb][:], bacc[cb], lean[cb][:], ADD)
+                nc.vector.tensor_tensor(yb[cb][:], wacc[cb], lean[cb][:], SUBTRACT)
             for cb in range(CB):
                 nc.vector.tensor_scalar(xa[:, cb, :], ya[cb][:], 0.0, 1.0, MAX, MIN)
                 nc.vector.tensor_scalar(xb[:, cb, :], yb[cb][:], 0.0, 1.0, MAX, MIN)
             return xa, xb
 
-        def first_layer(xa, xb):
-            h1 = acts.tile([P, MB, PW], BF16, name="h1")
+        def first_layer_group(h1, xa, xb, mb, pw):
+            units = slice(mb * P, (mb + 1) * P)
+            acc = psum.tile([P, pw], F32, name="acc")
+            for cb in range(CB):
+                nc.tensor.matmul(acc[:], w1a_sb[:, cb, units], xa[:, cb, :], start=(cb == 0), stop=False)
+            for cb in range(CB):
+                nc.tensor.matmul(acc[:], w1b_sb[:, cb, units], xb[:, cb, :], start=False, stop=(cb == CB - 1))
+            clip_out_of_psum(h1[:, mb, :], acc, one_less_b1[:, mb : mb + 1], pw)
+
+        def second_layer_piece(h1, j, p0, pw):
+            for units in range(QB_PER_PIECE):
+                qb = j * QB_PER_PIECE + units
+                acc = psum.tile([P, pw], F32, name="acc")
+                for mb in range(MB):
+                    weights = w2_sb[j][:, mb, units * P : (units + 1) * P]
+                    nc.tensor.matmul(acc[:], weights, h1[:, mb, :], start=(mb == 0), stop=(mb == MB - 1))
+                res = stage.tile([P, pw], F32, name="res")
+                clip_out_of_psum(res[:], acc, one_less_b2[:, qb : qb + 1], pw)
+                nc.sync.dma_start(out[qb * P : (qb + 1) * P, p0 : p0 + pw], res[:])
+
+        def hidden(k):
+            xa, xb = blended_inputs(starts[k], WIDTHS[k])
+            h1 = acts.tile([P, MB, WIDTHS[k]], BF16, name="h1")
             for mb in range(MB):
-                units = slice(mb * P, (mb + 1) * P)
-                acc = psum.tile([P, PW], F32, name="acc")
-                for cb in range(CB):
-                    nc.tensor.matmul(acc[:], w1a_sb[:, cb, units], xa[:, cb, :], start=(cb == 0), stop=False)
-                for cb in range(CB):
-                    nc.tensor.matmul(acc[:], w1b_sb[:, cb, units], xb[:, cb, :], start=False, stop=(cb == CB - 1))
-                clip_out_of_psum(h1[:, mb, :], acc, one_less_b1[:, mb : mb + 1])
+                first_layer_group(h1, xa, xb, mb, WIDTHS[k])
             return h1
 
-        def second_layer(h1, p0):
-            for qb in range(QB):
-                piece = w2_sb[qb // QB_PER_PIECE]
-                units = slice((qb % QB_PER_PIECE) * P, (qb % QB_PER_PIECE + 1) * P)
-                acc = psum.tile([P, PW], F32, name="acc")
-                for mb in range(MB):
-                    nc.tensor.matmul(acc[:], piece[:, mb, units], h1[:, mb, :], start=(mb == 0), stop=(mb == MB - 1))
-                res = stage.tile([P, PW], F32, name="res")
-                clip_out_of_psum(res[:], acc, one_less_b2[:, qb : qb + 1])
-                nc.sync.dma_start(out[qb * P : (qb + 1) * P, p0 : p0 + PW], res[:])
-
-        inputs = blended_inputs(0)
-        for p0 in range(0, B, PW):
-            h1 = first_layer(inputs[0], inputs[1])
-            if p0 + PW < B:
-                inputs = blended_inputs(p0 + PW)
-            second_layer(h1, p0)
+        starts = [sum(WIDTHS[:k]) for k in range(len(WIDTHS))]
+        h1 = [hidden(0)]
+        for j in range(LAG):
+            second_layer_piece(h1[0], j, starts[0], WIDTHS[0])
+        h1.append(hidden(1))
+        for j in range(LAG, W2_PIECES):
+            second_layer_piece(h1[0], j, starts[0], WIDTHS[0])
+            second_layer_piece(h1[1], j - LAG, starts[1], WIDTHS[1])
+        for j in range(W2_PIECES - LAG, W2_PIECES - 1):
+            second_layer_piece(h1[1], j, starts[1], WIDTHS[1])
+        for k in range(1, len(WIDTHS)):
+            if k + 1 < len(WIDTHS):
+                h1.append(hidden(k + 1))
+            second_layer_piece(h1[k], W2_PIECES - 1, starts[k], WIDTHS[k])
+            if k + 1 < len(WIDTHS):
+                for j in range(W2_PIECES - 1):
+                    second_layer_piece(h1[k + 1], j, starts[k + 1], WIDTHS[k + 1])

@@ -23,7 +23,7 @@ L3 = 2048
 CB = C // P
 MB = L2 // P
 QB = L3 // P
-WIDTHS = (96, 96, 128, 192)
+WIDTHS = (64, 64, 128, 256)
 LAG = 2
 WIDEST = max(WIDTHS)
 assert sum(WIDTHS) == B
@@ -41,7 +41,6 @@ def tile_halfkpnnue_b_kernel(tc, table, ft_bias, stm, w1a, w1b, b1, w2, b2, offs
         tc.tile_pool(name="ring", bufs=10) as ring,
         tc.tile_pool(name="acts", bufs=2) as acts,
         tc.tile_pool(name="rooms", bufs=4) as rooms,
-        tc.tile_pool(name="stage", bufs=8) as stage,
         tc.psum_pool(name="psum", bufs=8) as psum,
     ):
         offsets = held.tile([P, SIDES * SLOTS * B // 16], U16, name="offsets")
@@ -69,6 +68,8 @@ def tile_halfkpnnue_b_kernel(tc, table, ft_bias, stm, w1a, w1b, b1, w2, b2, offs
             piece = held.tile([P, MB, L3 // W2_PIECES], BF16, name="w2_%d" % j)
             nc.sync.dma_start(piece[:], w2_rows[:, :, j * (L3 // W2_PIECES) : (j + 1) * (L3 // W2_PIECES)])
             w2_sb.append(piece)
+
+        out_sb = held.tile([P, QB, B], F32, name="out_sb")
 
         nc.gpsimd.memset(bias_rows[MB + QB : BIAS_ROWS, :], 0.0)
         identity = held.tile([BIAS_ROWS, BIAS_ROWS], F32, name="identity")
@@ -135,9 +136,9 @@ def tile_halfkpnnue_b_kernel(tc, table, ft_bias, stm, w1a, w1b, b1, w2, b2, offs
                 for mb in range(MB):
                     weights = w2_sb[j][:, mb, units * P : (units + 1) * P]
                     nc.tensor.matmul(acc[:], weights, h1[:, mb, :], start=(mb == 0), stop=(mb == MB - 1))
-                res = stage.tile([P, pw], F32, name="res")
-                clip_out_of_psum(res[:], acc, one_less_b2[:, qb : qb + 1], pw)
-                nc.sync.dma_start(out[qb * P : (qb + 1) * P, p0 : p0 + pw], res[:])
+                res = out_sb[:, qb, p0 : p0 + pw]
+                clip_out_of_psum(res, acc, one_less_b2[:, qb : qb + 1], pw)
+                nc.sync.dma_start(out[qb * P : (qb + 1) * P, p0 : p0 + pw], res)
 
         def hidden(k):
             xa, xb = blended_inputs(starts[k], WIDTHS[k])

@@ -24,11 +24,16 @@ CB = C // P
 MB = L2 // P
 QB = L3 // P
 WIDTHS = (64, 64, 128, 256)
-LAG = 2
 WIDEST = max(WIDTHS)
+PAIR = WIDTHS[0] + WIDTHS[1]
 assert sum(WIDTHS) == B
 W2_PIECES = 4
 QB_PER_PIECE = QB // W2_PIECES
+BANKS = 8
+BANK_COLUMNS = 512
+QB_PER_BANK = BANK_COLUMNS // PAIR
+SHARED_BANKS = QB // QB_PER_BANK
+EARLY_ROWS = MB // 2
 BIAS_ROWS = 64
 
 FLOPS = 2 * B * (2 * C * L2 + L2 * L3)
@@ -41,7 +46,7 @@ def tile_halfkpnnue_b_kernel(tc, table, ft_bias, stm, w1a, w1b, b1, w2, b2, offs
         tc.tile_pool(name="ring", bufs=10) as ring,
         tc.tile_pool(name="acts", bufs=2) as acts,
         tc.tile_pool(name="rooms", bufs=4) as rooms,
-        tc.psum_pool(name="psum", bufs=8) as psum,
+        tc.psum_pool(name="psum", bufs=BANKS) as psum,
     ):
         offsets = held.tile([P, SIDES * SLOTS * B // 16], U16, name="offsets")
         nc.sync.dma_start(offsets[:], offs)
@@ -62,14 +67,14 @@ def tile_halfkpnnue_b_kernel(tc, table, ft_bias, stm, w1a, w1b, b1, w2, b2, offs
         bias_rows = held.tile([BIAS_ROWS, P], F32, name="bias_rows")
         nc.sync.dma_start(bias_rows[0:MB, :], b1.rearrange("(a p) o -> a (p o)", p=P))
         nc.sync.dma_start(bias_rows[MB : MB + QB, :], b2.rearrange("(a p) o -> a (p o)", p=P))
-        w2_rows = w2.rearrange("(mb p) q -> p mb q", p=P)
         w2_sb = []
-        for j in range(W2_PIECES):
-            piece = held.tile([P, MB, L3 // W2_PIECES], BF16, name="w2_%d" % j)
-            nc.sync.dma_start(piece[:], w2_rows[:, :, j * (L3 // W2_PIECES) : (j + 1) * (L3 // W2_PIECES)])
-            w2_sb.append(piece)
+        for mb in range(MB):
+            rows = held.tile([P, L3], BF16, name="w2_%d" % mb)
+            nc.sync.dma_start(rows[:], w2[mb * P : (mb + 1) * P, :])
+            w2_sb.append(rows)
 
         out_sb = held.tile([P, QB, B], F32, name="out_sb")
+        h1 = held.tile([P, MB, B], BF16, name="h1")
 
         nc.gpsimd.memset(bias_rows[MB + QB : BIAS_ROWS, :], 0.0)
         identity = held.tile([BIAS_ROWS, BIAS_ROWS], F32, name="identity")
@@ -120,47 +125,79 @@ def tile_halfkpnnue_b_kernel(tc, table, ft_bias, stm, w1a, w1b, b1, w2, b2, offs
                 nc.vector.tensor_scalar(xb[:, cb, :], yb[cb][:], 0.0, 1.0, MAX, MIN)
             return xa, xb
 
-        def first_layer_group(h1, xa, xb, mb, pw):
+        def first_layer_group(xa, xb, mb, p0, pw):
             units = slice(mb * P, (mb + 1) * P)
             acc = psum.tile([P, pw], F32, name="acc")
             for cb in range(CB):
                 nc.tensor.matmul(acc[:], w1a_sb[:, cb, units], xa[:, cb, :], start=(cb == 0), stop=False)
             for cb in range(CB):
                 nc.tensor.matmul(acc[:], w1b_sb[:, cb, units], xb[:, cb, :], start=False, stop=(cb == CB - 1))
-            clip_out_of_psum(h1[:, mb, :], acc, one_less_b1[:, mb : mb + 1], pw)
+            clip_out_of_psum(h1[:, mb, p0 : p0 + pw], acc, one_less_b1[:, mb : mb + 1], pw)
 
-        def second_layer_piece(h1, j, p0, pw):
+        def second_layer_piece(j, p0, pw):
             for units in range(QB_PER_PIECE):
                 qb = j * QB_PER_PIECE + units
                 acc = psum.tile([P, pw], F32, name="acc")
                 for mb in range(MB):
-                    weights = w2_sb[j][:, mb, units * P : (units + 1) * P]
-                    nc.tensor.matmul(acc[:], weights, h1[:, mb, :], start=(mb == 0), stop=(mb == MB - 1))
+                    weights = w2_sb[mb][:, qb * P : (qb + 1) * P]
+                    nc.tensor.matmul(acc[:], weights, h1[:, mb, p0 : p0 + pw], start=(mb == 0), stop=(mb == MB - 1))
                 res = out_sb[:, qb, p0 : p0 + pw]
                 clip_out_of_psum(res, acc, one_less_b2[:, qb : qb + 1], pw)
                 nc.sync.dma_start(out[qb * P : (qb + 1) * P, p0 : p0 + pw], res)
 
-        def hidden(k):
+        def first_layer(k):
             xa, xb = blended_inputs(starts[k], WIDTHS[k])
-            h1 = acts.tile([P, MB, WIDTHS[k]], BF16, name="h1")
             for mb in range(MB):
-                first_layer_group(h1, xa, xb, mb, WIDTHS[k])
-            return h1
+                first_layer_group(xa, xb, mb, starts[k], WIDTHS[k])
+
+
+        def second_layer_early_rows(k):
+            for mb in range(EARLY_ROWS):
+                for qb in range(QB):
+                    bank, place = divmod(qb, QB_PER_BANK)
+                    nc.tensor.matmul(
+                        shared[bank][:, place, starts[k] : starts[k] + WIDTHS[k]],
+                        w2_sb[mb][:, qb * P : (qb + 1) * P],
+                        h1[:, mb, starts[k] : starts[k] + WIDTHS[k]],
+                        start=(k == 0 and mb == 0 and place == 0),
+                        stop=False,
+                    )
+
+        def second_layer_rest_of_bank(bank):
+            for place in range(QB_PER_BANK):
+                qb = bank * QB_PER_BANK + place
+                for mb in range(EARLY_ROWS, MB):
+                    nc.tensor.matmul(
+                        shared[bank][:, place, :],
+                        w2_sb[mb][:, qb * P : (qb + 1) * P],
+                        h1[:, mb, 0:PAIR],
+                        start=False,
+                        stop=(place == QB_PER_BANK - 1 and mb == MB - 1),
+                    )
+            for place in range(QB_PER_BANK):
+                qb = bank * QB_PER_BANK + place
+                res = out_sb[:, qb, 0:PAIR]
+                room = rooms.tile([P, PAIR], F32, name="room")
+                nc.scalar.activation(room[:], shared[bank][:, place, :], RELU, bias=one_less_b2[:, qb : qb + 1], scale=-1.0)
+                nc.scalar.activation(res, room[:], RELU, bias=1.0, scale=-1.0)
+                nc.sync.dma_start(out[qb * P : (qb + 1) * P, 0:PAIR], res)
 
         starts = [sum(WIDTHS[:k]) for k in range(len(WIDTHS))]
-        h1 = [hidden(0)]
-        for j in range(LAG):
-            second_layer_piece(h1[0], j, starts[0], WIDTHS[0])
-        h1.append(hidden(1))
-        for j in range(LAG, W2_PIECES):
-            second_layer_piece(h1[0], j, starts[0], WIDTHS[0])
-            second_layer_piece(h1[1], j - LAG, starts[1], WIDTHS[1])
-        for j in range(W2_PIECES - LAG, W2_PIECES - 1):
-            second_layer_piece(h1[1], j, starts[1], WIDTHS[1])
-        for k in range(1, len(WIDTHS)):
+        LAST = W2_PIECES - 1
+        first_layer(0)
+        shared = [
+            psum.tile([P, QB_PER_BANK, PAIR], F32, name="shared%d" % bank, tag="acc") for bank in range(SHARED_BANKS)
+        ]
+        second_layer_early_rows(0)
+        first_layer(1)
+        second_layer_early_rows(1)
+        for bank in range(SHARED_BANKS - 1):
+            second_layer_rest_of_bank(bank)
+        first_layer(2)
+        second_layer_rest_of_bank(SHARED_BANKS - 1)
+        for k in (2, 3):
+            for j in range(LAST):
+                second_layer_piece(j, starts[k], WIDTHS[k])
             if k + 1 < len(WIDTHS):
-                h1.append(hidden(k + 1))
-            second_layer_piece(h1[k], W2_PIECES - 1, starts[k], WIDTHS[k])
-            if k + 1 < len(WIDTHS):
-                for j in range(W2_PIECES - 1):
-                    second_layer_piece(h1[k + 1], j, starts[k + 1], WIDTHS[k + 1])
+                first_layer(k + 1)
+            second_layer_piece(LAST, starts[k], WIDTHS[k])

@@ -23,7 +23,7 @@ L3 = 2048
 CB = C // P
 MB = L2 // P
 QB = L3 // P
-WIDTHS = (64, 64, 128, 256)
+WIDTHS = (64, 64, 160, 224)
 WIDEST = max(WIDTHS)
 PAIR = WIDTHS[0] + WIDTHS[1]
 assert sum(WIDTHS) == B

@@ -34,6 +34,9 @@ BANK_COLUMNS = 512
 QB_PER_BANK = BANK_COLUMNS // PAIR
 SHARED_BANKS = QB // QB_PER_BANK
 EARLY_ROWS = MB // 2
+QB_PER_STEP = QB * EARLY_ROWS // MB
+BEHIND = 2
+LAST_ROWS = 5
 BIAS_ROWS = 64
 
 FLOPS = 2 * B * (2 * C * L2 + L2 * L3)
@@ -151,22 +154,42 @@ def tile_halfkpnnue_b_kernel(tc, table, ft_bias, stm, w1a, w1b, b1, w2, b2, offs
                 first_layer_group(xa, xb, mb, starts[k], WIDTHS[k])
 
 
-        def second_layer_early_rows(k):
-            for mb in range(EARLY_ROWS):
+        def early_products(k, first):
+            for number in range(first, first + QB_PER_STEP):
+                mb, qb = divmod(number, QB)
+                bank, place = divmod(qb, QB_PER_BANK)
+                nc.tensor.matmul(
+                    shared[bank][:, place, starts[k] : starts[k] + WIDTHS[k]],
+                    w2_sb[mb][:, qb * P : (qb + 1) * P],
+                    h1[:, mb, starts[k] : starts[k] + WIDTHS[k]],
+                    start=(k == 0 and mb == 0 and place == 0),
+                    stop=False,
+                )
+
+        def first_layer_with_early_products(k):
+            xa, xb = blended_inputs(starts[k], WIDTHS[k])
+            for step in range(MB + BEHIND):
+                if step < MB:
+                    first_layer_group(xa, xb, step, starts[k], WIDTHS[k])
+                if step >= BEHIND:
+                    early_products(k, (step - BEHIND) * QB_PER_STEP)
+
+        def middle_products():
+            for mb in range(EARLY_ROWS, MB - LAST_ROWS):
                 for qb in range(QB):
                     bank, place = divmod(qb, QB_PER_BANK)
                     nc.tensor.matmul(
-                        shared[bank][:, place, starts[k] : starts[k] + WIDTHS[k]],
+                        shared[bank][:, place, :],
                         w2_sb[mb][:, qb * P : (qb + 1) * P],
-                        h1[:, mb, starts[k] : starts[k] + WIDTHS[k]],
-                        start=(k == 0 and mb == 0 and place == 0),
+                        h1[:, mb, 0:PAIR],
+                        start=False,
                         stop=False,
                     )
 
         def second_layer_rest_of_bank(bank):
             for place in range(QB_PER_BANK):
                 qb = bank * QB_PER_BANK + place
-                for mb in range(EARLY_ROWS, MB):
+                for mb in range(MB - LAST_ROWS, MB):
                     nc.tensor.matmul(
                         shared[bank][:, place, :],
                         w2_sb[mb][:, qb * P : (qb + 1) * P],
@@ -188,9 +211,10 @@ def tile_halfkpnnue_b_kernel(tc, table, ft_bias, stm, w1a, w1b, b1, w2, b2, offs
         shared = [
             psum.tile([P, QB_PER_BANK, PAIR], F32, name="shared%d" % bank, tag="acc") for bank in range(SHARED_BANKS)
         ]
-        second_layer_early_rows(0)
-        first_layer(1)
-        second_layer_early_rows(1)
+        for step in range(MB):
+            early_products(0, step * QB_PER_STEP)
+        first_layer_with_early_products(1)
+        middle_products()
         for bank in range(SHARED_BANKS - 1):
             second_layer_rest_of_bank(bank)
         first_layer(2)

@@ -37,6 +37,7 @@ EARLY_ROWS = MB // 2
 QB_PER_STEP = QB * EARLY_ROWS // MB
 BEHIND = 2
 LAST_ROWS = 5
+SHORT_END = 64
 BIAS_ROWS = 64
 
 FLOPS = 2 * B * (2 * C * L2 + L2 * L3)
@@ -137,16 +138,18 @@ def tile_halfkpnnue_b_kernel(tc, table, ft_bias, stm, w1a, w1b, b1, w2, b2, offs
                 nc.tensor.matmul(acc[:], w1b_sb[:, cb, units], xb[:, cb, :], start=False, stop=(cb == CB - 1))
             clip_out_of_psum(h1[:, mb, p0 : p0 + pw], acc, one_less_b1[:, mb : mb + 1], pw)
 
+        def second_layer_group(qb, p0, pw):
+            acc = psum.tile([P, pw], F32, name="acc")
+            for mb in range(MB):
+                weights = w2_sb[mb][:, qb * P : (qb + 1) * P]
+                nc.tensor.matmul(acc[:], weights, h1[:, mb, p0 : p0 + pw], start=(mb == 0), stop=(mb == MB - 1))
+            res = out_sb[:, qb, p0 : p0 + pw]
+            clip_out_of_psum(res, acc, one_less_b2[:, qb : qb + 1], pw)
+            nc.sync.dma_start(out[qb * P : (qb + 1) * P, p0 : p0 + pw], res)
+
         def second_layer_piece(j, p0, pw):
-            for units in range(QB_PER_PIECE):
-                qb = j * QB_PER_PIECE + units
-                acc = psum.tile([P, pw], F32, name="acc")
-                for mb in range(MB):
-                    weights = w2_sb[mb][:, qb * P : (qb + 1) * P]
-                    nc.tensor.matmul(acc[:], weights, h1[:, mb, p0 : p0 + pw], start=(mb == 0), stop=(mb == MB - 1))
-                res = out_sb[:, qb, p0 : p0 + pw]
-                clip_out_of_psum(res, acc, one_less_b2[:, qb : qb + 1], pw)
-                nc.sync.dma_start(out[qb * P : (qb + 1) * P, p0 : p0 + pw], res)
+            for qb in range(j * QB_PER_PIECE, (j + 1) * QB_PER_PIECE):
+                second_layer_group(qb, p0, pw)
 
         def first_layer(k):
             xa, xb = blended_inputs(starts[k], WIDTHS[k])
@@ -219,9 +222,11 @@ def tile_halfkpnnue_b_kernel(tc, table, ft_bias, stm, w1a, w1b, b1, w2, b2, offs
             second_layer_rest_of_bank(bank)
         first_layer(2)
         second_layer_rest_of_bank(SHARED_BANKS - 1)
-        for k in (2, 3):
-            for j in range(LAST):
-                second_layer_piece(j, starts[k], WIDTHS[k])
-            if k + 1 < len(WIDTHS):
-                first_layer(k + 1)
-            second_layer_piece(LAST, starts[k], WIDTHS[k])
+        for j in range(LAST):
+            second_layer_piece(j, starts[2], WIDTHS[2])
+        first_layer(3)
+        second_layer_piece(LAST, starts[2], WIDTHS[2])
+        for qb in range(QB - 1):
+            second_layer_group(qb, starts[3], WIDTHS[3])
+        second_layer_group(QB - 1, starts[3], WIDTHS[3] - SHORT_END)
+        second_layer_group(QB - 1, B - SHORT_END, SHORT_END)

@@ -147,9 +147,28 @@ def tile_halfkpnnue_b_kernel(tc, table, ft_bias, stm, w1a, w1b, b1, w2, b2, offs
             clip_out_of_psum(res, acc, one_less_b2[:, qb : qb + 1], pw)
             nc.sync.dma_start(out[qb * P : (qb + 1) * P, p0 : p0 + pw], res)
 
-        def second_layer_piece(j, p0, pw):
-            for qb in range(j * QB_PER_PIECE, (j + 1) * QB_PER_PIECE):
-                second_layer_group(qb, p0, pw)
+        def second_layer_blocks(blocks, p0, pw):
+            per_bank = BANK_COLUMNS // pw
+            for first in range(0, len(blocks), per_bank):
+                together = blocks[first : first + per_bank]
+                acc = psum.tile([P, per_bank, pw], F32, name="acc")
+                for place in range(len(together)):
+                    qb = together[place]
+                    for mb in range(MB):
+                        nc.tensor.matmul(
+                            acc[:, place, :],
+                            w2_sb[mb][:, qb * P : (qb + 1) * P],
+                            h1[:, mb, p0 : p0 + pw],
+                            start=(place == 0 and mb == 0),
+                            stop=(place == len(together) - 1 and mb == MB - 1),
+                        )
+                for place in range(len(together)):
+                    qb = together[place]
+                    res = out_sb[:, qb, p0 : p0 + pw]
+                    room = rooms.tile([P, pw], F32, name="room")
+                    nc.scalar.activation(room[:], acc[:, place, :], RELU, bias=one_less_b2[:, qb : qb + 1], scale=-1.0)
+                    nc.scalar.activation(res, room[:], RELU, bias=1.0, scale=-1.0)
+                    nc.sync.dma_start(out[qb * P : (qb + 1) * P, p0 : p0 + pw], res)
 
         def first_layer(k):
             xa, xb = blended_inputs(starts[k], WIDTHS[k])
@@ -222,11 +241,9 @@ def tile_halfkpnnue_b_kernel(tc, table, ft_bias, stm, w1a, w1b, b1, w2, b2, offs
             second_layer_rest_of_bank(bank)
         first_layer(2)
         second_layer_rest_of_bank(SHARED_BANKS - 1)
-        for j in range(LAST):
-            second_layer_piece(j, starts[2], WIDTHS[2])
+        second_layer_blocks(list(range(LAST * QB_PER_PIECE)), starts[2], WIDTHS[2])
         first_layer(3)
-        second_layer_piece(LAST, starts[2], WIDTHS[2])
-        for qb in range(QB - 1):
-            second_layer_group(qb, starts[3], WIDTHS[3])
+        second_layer_blocks(list(range(LAST * QB_PER_PIECE, QB)), starts[2], WIDTHS[2])
+        second_layer_blocks(list(range(QB - 1)), starts[3], WIDTHS[3])
         second_layer_group(QB - 1, starts[3], WIDTHS[3] - SHORT_END)
         second_layer_group(QB - 1, B - SHORT_END, SHORT_END)

import concourse.mybir as mybir
from concourse.masks import make_identity

F32 = mybir.dt.float32
BF16 = mybir.dt.bfloat16
U16 = mybir.dt.uint16
ADD = mybir.AluOpType.add
SUBTRACT = mybir.AluOpType.subtract
MULT = mybir.AluOpType.mult
MAX = mybir.AluOpType.max
MIN = mybir.AluOpType.min
RELU = mybir.ActivationFunctionType.Relu
COPY = mybir.ActivationFunctionType.Copy

P = 128
C = 256
S = 1024
B = 512
SIDES = 2
SLOTS = 8
L2 = 2048
L3 = 2048
CB = C // P
MB = L2 // P
QB = L3 // P
WIDTHS = (64, 64, 160, 224)
WIDEST = max(WIDTHS)
PAIR = WIDTHS[0] + WIDTHS[1]
assert sum(WIDTHS) == B
W2_PIECES = 4
QB_PER_PIECE = QB // W2_PIECES
BANKS = 8
BANK_COLUMNS = 512
QB_PER_BANK = BANK_COLUMNS // PAIR
SHARED_BANKS = QB // QB_PER_BANK
EARLY_ROWS = MB // 2
QB_PER_STEP = QB * EARLY_ROWS // MB
BEHIND = 2
LAST_ROWS = 5
SHORT_END = 64
BIAS_ROWS = 64

FLOPS = 2 * B * (2 * C * L2 + L2 * L3)


def tile_halfkpnnue_b_kernel(tc, table, ft_bias, stm, w1a, w1b, b1, w2, b2, offs, out):
    nc = tc.nc
    with (
        tc.tile_pool(name="held", bufs=1) as held,
        tc.tile_pool(name="ring", bufs=10) as ring,
        tc.tile_pool(name="acts", bufs=2) as acts,
        tc.tile_pool(name="rooms", bufs=4) as rooms,
        tc.psum_pool(name="psum", bufs=BANKS) as psum,
    ):
        offsets = held.tile([P, SIDES * SLOTS * B // 16], U16, name="offsets")
        nc.sync.dma_start(offsets[:], offs)
        ft_sb = held.tile([P, CB], F32, name="ft_sb")
        with nc.allow_non_contiguous_dma(reason="256 values, one to a partition"):
            nc.sync.dma_start(ft_sb[:], ft_bias.rearrange("(a p) o -> p (a o)", p=P))
        table_sb = []
        for cb in range(CB):
            block = held.tile([P, S], F32, name="table%d" % cb)
            nc.sync.dma_start(block[:], table[cb * P : (cb + 1) * P, :])
            table_sb.append(block)
        stm_sb = held.tile([P, B], F32, name="stm_sb")
        nc.sync.dma_start(stm_sb[:], stm.rearrange("o b -> (o b)").partition_broadcast(P))
        w1a_sb = held.tile([P, CB, L2], BF16, name="w1a_sb")
        nc.sync.dma_start(w1a_sb[:], w1a.rearrange("(cb p) m -> p cb m", p=P))
        w1b_sb = held.tile([P, CB, L2], BF16, name="w1b_sb")
        nc.sync.dma_start(w1b_sb[:], w1b.rearrange("(cb p) m -> p cb m", p=P))
        bias_rows = held.tile([BIAS_ROWS, P], F32, name="bias_rows")
        nc.sync.dma_start(bias_rows[0:MB, :], b1.rearrange("(a p) o -> a (p o)", p=P))
        nc.sync.dma_start(bias_rows[MB : MB + QB, :], b2.rearrange("(a p) o -> a (p o)", p=P))
        w2_sb = []
        for mb in range(MB):
            rows = held.tile([P, L3], BF16, name="w2_%d" % mb)
            nc.sync.dma_start(rows[:], w2[mb * P : (mb + 1) * P, :])
            w2_sb.append(rows)

        out_sb = held.tile([P, QB, B], F32, name="out_sb")
        h1 = held.tile([P, MB, B], BF16, name="h1")

        nc.gpsimd.memset(bias_rows[MB + QB : BIAS_ROWS, :], 0.0)
        identity = held.tile([BIAS_ROWS, BIAS_ROWS], F32, name="identity")
        make_identity(nc, identity[:])
        bias_ps = psum.tile([P, BIAS_ROWS], F32, tag="acc")
        nc.tensor.transpose(bias_ps[:], bias_rows[:], identity[:])
        one_less_bias = held.tile([P, BIAS_ROWS], F32, name="one_less_bias")
        nc.scalar.activation(one_less_bias[:], bias_ps[:], COPY, bias=1.0, scale=-1.0)
        one_less_b1 = one_less_bias[:, 0:MB]
        one_less_b2 = one_less_bias[:, MB : MB + QB]

        def clip_out_of_psum(clipped, acc, one_less_b, pw):
            room = rooms.tile([P, pw], F32, name="room")
            nc.scalar.activation(room[:], acc[:], RELU, bias=one_less_b, scale=-1.0)
            nc.scalar.activation(clipped, room[:], RELU, bias=1.0, scale=-1.0)

        bias_start = []
        for cb in range(CB):
            spread = held.tile([P, WIDEST], F32, name="bias_start%d" % cb)
            nc.vector.tensor_copy(spread[:], ft_sb[:, cb : cb + 1].to_broadcast([P, WIDEST]))
            bias_start.append(spread)

        def blended_inputs(p0, pw):
            bags = [[bias_start[cb][:, 0:pw] for cb in range(CB)] for side in range(SIDES)]
            for t in range(SLOTS):
                for side in range(SIDES):
                    first = ((side * SLOTS + t) * B + p0) // 16
                    for cb in range(CB):
                        picked = table_sb[cb][:].indirect(offsets[:, first : first + pw // 16])
                        longer = ring.tile([P, pw], F32, name="longer", tag="vector")
                        nc.vector.tensor_tensor(longer[:], picked, bags[side][cb], ADD)
                        bags[side][cb] = longer[:]
            wacc, bacc = bags
            lean = [ring.tile([P, pw], F32, name="lean%d" % cb, tag="vector") for cb in range(CB)]
            ya = [ring.tile([P, pw], F32, name="ya%d" % cb, tag="vector") for cb in range(CB)]
            yb = [ring.tile([P, pw], F32, name="yb%d" % cb, tag="vector") for cb in range(CB)]
            xa = acts.tile([P, CB, pw], BF16, name="xa")
            xb = acts.tile([P, CB, pw], BF16, name="xb")
            for cb in range(CB):
                nc.vector.tensor_tensor(lean[cb][:], wacc[cb], bacc[cb], SUBTRACT)
            for cb in range(CB):
                nc.vector.tensor_tensor(lean[cb][:], lean[cb][:], stm_sb[:, p0 : p0 + pw], MULT)
            for cb in range(CB):
                nc.vector.tensor_tensor(ya[cb][:], bacc[cb], lean[cb][:], ADD)
                nc.vector.tensor_tensor(yb[cb][:], wacc[cb], lean[cb][:], SUBTRACT)
            for cb in range(CB):
                nc.vector.tensor_scalar(xa[:, cb, :], ya[cb][:], 0.0, 1.0, MAX, MIN)
                nc.vector.tensor_scalar(xb[:, cb, :], yb[cb][:], 0.0, 1.0, MAX, MIN)
            return xa, xb

        def first_layer_group(xa, xb, mb, p0, pw):
            units = slice(mb * P, (mb + 1) * P)
            acc = psum.tile([P, pw], F32, name="acc")
            for cb in range(CB):
                nc.tensor.matmul(acc[:], w1a_sb[:, cb, units], xa[:, cb, :], start=(cb == 0), stop=False)
            for cb in range(CB):
                nc.tensor.matmul(acc[:], w1b_sb[:, cb, units], xb[:, cb, :], start=False, stop=(cb == CB - 1))
            clip_out_of_psum(h1[:, mb, p0 : p0 + pw], acc, one_less_b1[:, mb : mb + 1], pw)

        def second_layer_group(qb, p0, pw):
            acc = psum.tile([P, pw], F32, name="acc")
            for mb in range(MB):
                weights = w2_sb[mb][:, qb * P : (qb + 1) * P]
                nc.tensor.matmul(acc[:], weights, h1[:, mb, p0 : p0 + pw], start=(mb == 0), stop=(mb == MB - 1))
            res = out_sb[:, qb, p0 : p0 + pw]
            clip_out_of_psum(res, acc, one_less_b2[:, qb : qb + 1], pw)
            nc.sync.dma_start(out[qb * P : (qb + 1) * P, p0 : p0 + pw], res)

        def second_layer_blocks(blocks, p0, pw):
            per_bank = BANK_COLUMNS // pw
            for first in range(0, len(blocks), per_bank):
                together = blocks[first : first + per_bank]
                acc = psum.tile([P, per_bank, pw], F32, name="acc")
                for place in range(len(together)):
                    qb = together[place]
                    for mb in range(MB):
                        nc.tensor.matmul(
                            acc[:, place, :],
                            w2_sb[mb][:, qb * P : (qb + 1) * P],
                            h1[:, mb, p0 : p0 + pw],
                            start=(place == 0 and mb == 0),
                            stop=(place == len(together) - 1 and mb == MB - 1),
                        )
                for place in range(len(together)):
                    qb = together[place]
                    res = out_sb[:, qb, p0 : p0 + pw]
                    room = rooms.tile([P, pw], F32, name="room")
                    nc.scalar.activation(room[:], acc[:, place, :], RELU, bias=one_less_b2[:, qb : qb + 1], scale=-1.0)
                    nc.scalar.activation(res, room[:], RELU, bias=1.0, scale=-1.0)
                    nc.sync.dma_start(out[qb * P : (qb + 1) * P, p0 : p0 + pw], res)

        def first_layer(k):
            xa, xb = blended_inputs(starts[k], WIDTHS[k])
            for mb in range(MB):
                first_layer_group(xa, xb, mb, starts[k], WIDTHS[k])


        def early_products(k, first):
            for number in range(first, first + QB_PER_STEP):
                mb, qb = divmod(number, QB)
                bank, place = divmod(qb, QB_PER_BANK)
                nc.tensor.matmul(
                    shared[bank][:, place, starts[k] : starts[k] + WIDTHS[k]],
                    w2_sb[mb][:, qb * P : (qb + 1) * P],
                    h1[:, mb, starts[k] : starts[k] + WIDTHS[k]],
                    start=(k == 0 and mb == 0 and place == 0),
                    stop=False,
                )

        def first_layer_with_early_products(k):
            xa, xb = blended_inputs(starts[k], WIDTHS[k])
            for step in range(MB + BEHIND):
                if step < MB:
                    first_layer_group(xa, xb, step, starts[k], WIDTHS[k])
                if step >= BEHIND:
                    early_products(k, (step - BEHIND) * QB_PER_STEP)

        def middle_products():
            for mb in range(EARLY_ROWS, MB - LAST_ROWS):
                for qb in range(QB):
                    bank, place = divmod(qb, QB_PER_BANK)
                    nc.tensor.matmul(
                        shared[bank][:, place, :],
                        w2_sb[mb][:, qb * P : (qb + 1) * P],
                        h1[:, mb, 0:PAIR],
                        start=False,
                        stop=False,
                    )

        def second_layer_rest_of_bank(bank):
            for place in range(QB_PER_BANK):
                qb = bank * QB_PER_BANK + place
                for mb in range(MB - LAST_ROWS, MB):
                    nc.tensor.matmul(
                        shared[bank][:, place, :],
                        w2_sb[mb][:, qb * P : (qb + 1) * P],
                        h1[:, mb, 0:PAIR],
                        start=False,
                        stop=(place == QB_PER_BANK - 1 and mb == MB - 1),
                    )
            for place in range(QB_PER_BANK):
                qb = bank * QB_PER_BANK + place
                res = out_sb[:, qb, 0:PAIR]
                room = rooms.tile([P, PAIR], F32, name="room")
                nc.scalar.activation(room[:], shared[bank][:, place, :], RELU, bias=one_less_b2[:, qb : qb + 1], scale=-1.0)
                nc.scalar.activation(res, room[:], RELU, bias=1.0, scale=-1.0)
                nc.sync.dma_start(out[qb * P : (qb + 1) * P, 0:PAIR], res)

        starts = [sum(WIDTHS[:k]) for k in range(len(WIDTHS))]
        LAST = W2_PIECES - 1
        first_layer(0)
        shared = [
            psum.tile([P, QB_PER_BANK, PAIR], F32, name="shared%d" % bank, tag="acc") for bank in range(SHARED_BANKS)
        ]
        for step in range(MB):
            early_products(0, step * QB_PER_STEP)
        first_layer_with_early_products(1)
        middle_products()
        for bank in range(SHARED_BANKS - 1):
            second_layer_rest_of_bank(bank)
        first_layer(2)
        second_layer_rest_of_bank(SHARED_BANKS - 1)
        second_layer_blocks(list(range(LAST * QB_PER_PIECE)), starts[2], WIDTHS[2])
        first_layer(3)
        second_layer_blocks(list(range(LAST * QB_PER_PIECE, QB)), starts[2], WIDTHS[2])
        second_layer_blocks(list(range(QB - 1)), starts[3], WIDTHS[3])
        second_layer_group(QB - 1, starts[3], WIDTHS[3] - SHORT_END)
        second_layer_group(QB - 1, B - SHORT_END, SHORT_END)
